import numpy as np
import ml_dtypes


def mxq(x, axis, fmt="e4m3"):
    dtype, down = {"e4m3": (ml_dtypes.float8_e4m3fn, 7), "e5m2": (ml_dtypes.float8_e5m2, 14)}[fmt]
    v = np.moveaxis(np.asarray(x, np.float32).astype(ml_dtypes.bfloat16).astype(np.float64), axis, -1)
    blocks = v.reshape(v.shape[:-1] + (-1, 32))
    amax = np.abs(blocks).max(-1, keepdims=True)
    byte = np.maximum(np.where(amax > 0, np.frexp(amax)[1] - 1 + 127, 0) - down, 1)
    scale = np.exp2(byte - 127.0)
    codes = (blocks / scale).astype(np.float32).astype(dtype).astype(np.float64)
    return np.moveaxis((codes * scale).reshape(v.shape), -1, axis)


WIDE = False


def mx_kscale(k):
    if not WIDE:
        return np.ones(k)
    levels = np.array([10, -10, 5, -5, 0])
    if k % 512:
        return np.exp2(np.random.permutation(np.resize(levels, k // 32))).repeat(32)
    a = np.empty((k // 512, 16))
    for p in range(k // 512):
        a[p, :8] = np.random.permutation(np.resize(levels, 8))
        for g in range(8):
            far = levels[np.abs(levels - a[p, g]) >= 10]
            a[p, g + 8] = far[np.random.randint(len(far))]
    return np.exp2(a.ravel()).repeat(32)


BF16 = ml_dtypes.bfloat16


def bf(x):
    return np.asarray(x, np.float32).astype(BF16)


def f64(x):
    return np.asarray(x).astype(np.float64)


B, N, C = 8, 1024, 256
Q = N ** 0.25


def setup_inputs():
    s = mx_kscale(N)
    msg = (1.4 * np.random.standard_normal((B, 1, C)) + 1.2 * np.random.standard_normal((B, N, C))) / Q
    return {"A": bf(np.random.uniform(0.0, 1.0, (B, N, N)) * 2.0 / N ** 0.75 * s),
            "msg": bf(msg / s[:, None]),
            "h": bf(np.maximum(np.random.standard_normal((B, N, C)) * 1.35, 0.0)),
            "Ws": bf(np.random.uniform(-1.0, 1.0, (C, C)) * 1.5 / np.sqrt(C)),
            "b": bf(np.random.uniform(-1.0, 1.0, C) * 0.5)}


def reference(A, msg, h, Ws, b):
    agg = mxq(f64(A), 2, "e4m3") @ mxq(f64(msg), 1, "e4m3")
    return np.maximum(agg + f64(h) @ f64(Ws).T + f64(b), 0.0)

@@ -1,0 +1,249 @@
+from contextlib import ExitStack
+
+import concourse.mybir as mybir
+from concourse.masks import make_identity
+
+FLOPS = 2 * 8 * 1024 * 256 * (1024 + 256)
+
+F32 = mybir.dt.float32
+BF16 = mybir.dt.bfloat16
+U32 = mybir.dt.uint32
+U8 = mybir.dt.uint8
+FP8X4 = mybir.dt.float8_e4m3fn_x4
+ADD = mybir.AluOpType.add
+MULT = mybir.AluOpType.mult
+RELU = mybir.ActivationFunctionType.Relu
+P = 128
+AHEAD = 3
+ST_LAG = 4
+WEAVE = True
+V_GRAPHS = 2
+
+
+def tile_gcnstacking_pb_t_kernel(tc, A, msg, h, Ws, b, out):
+    nc = tc.nc
+    G = 8
+    NQ = 2 * G
+
+    a_view = A.rearrange("g (p q t) k -> g q p (t k)", p=P, q=2, t=4)
+    o_view = out.rearrange("g (p q t) c -> g q p (t c)", p=P, q=2, t=4)
+    h_view = h.rearrange("g (p r) c -> g p (r c)", p=P)
+    m_view = msg.rearrange("g (c p t) n -> g p c (t n)", c=2, p=P, t=4)
+
+    with ExitStack() as ctx:
+        const = ctx.enter_context(tc.tile_pool(name="const", bufs=1))
+        raw = ctx.enter_context(tc.tile_pool(name="raw", bufs=4))
+        work = ctx.enter_context(tc.tile_pool(name="work", bufs=3))
+        psum = ctx.enter_context(tc.psum_pool(name="psum", bufs=1))
+        ctx.enter_context(tc.manual_schedule())
+
+        a_raw, h_raw, m_raw = {}, {}, {}
+        a_grp, a_cod, a_scl = {}, {}, {}
+        m_grp, m_cod, m_scl = {}, {}, {}
+        hT, y = {}, {}
+
+        def load_msg(g):
+            m_raw[g] = raw.tile([P, 2048], BF16, name="m_raw", tag="m_raw", bufs=AHEAD + 2)
+            nc.sync.dma_start(out=m_raw[g][:].rearrange("p (c x) -> p c x", c=2), in_=m_view[g])
+
+        def load_graph(g):
+            a_raw[2 * g] = raw.tile([P, 4096], BF16, name="a_raw", tag="a_raw", bufs=2 * (AHEAD + 1))
+            h_raw[g] = raw.tile([P, 2048], BF16, name="h_raw", tag="h_raw", bufs=AHEAD + 1)
+            a_raw[2 * g + 1] = raw.tile([P, 4096], BF16, name="a_raw", tag="a_raw", bufs=2 * (AHEAD + 1))
+            if g == 0:
+                for t in range(4):
+                    nc.sync.dma_start(out=a_raw[0][:, 1024 * t:1024 * (t + 1)], in_=a_view[0, 0][:, 1024 * t:1024 * (t + 1)])
+                nc.sync.dma_start(out=h_raw[g][:], in_=h_view[g])
+                load_msg(0)
+            else:
+                if g == 2:
+                    load_msg(2)
+                nc.sync.dma_start(out=a_raw[2 * g][:], in_=a_view[g, 0])
+                if g == 1:
+                    load_msg(1)
+                elif g + 1 < G:
+                    load_msg(g + 1)
+                nc.sync.dma_start(out=h_raw[g][:], in_=h_view[g])
+            nc.sync.dma_start(out=a_raw[2 * g + 1][:], in_=a_view[g, 1])
+
+        def a_tile_steps(j, t):
+            words = a_raw[j][:].bitcast(F32)
+            grp_words = a_grp[j][:].bitcast(F32)
+            bank = psum.tile([P, 512], F32, name="at", tag="at", bufs=4)
+
+            def one(s):
+                c, u = divmod(s, 2)
+                lo = 512 * t + 256 * c
+                nc.tensor.transpose(out=bank[:, 128 * s:128 * (s + 1)], in_=words[:, lo + u:lo + 256:2], identity=ident[:])
+                if s == 3:
+                    nc.scalar.copy(
+                        out=grp_words[:, 512 * t:512 * (t + 1)].rearrange("p (c i u) -> p c i u", c=2, i=128, u=2),
+                        in_=bank[:].rearrange("p (c u i) -> p c i u", c=2, u=2, i=128),
+                    )
+
+            return [(one, s) for s in range(4)]
+
+        def h_steps(j):
+            g, q = divmod(j, 2)
+            h_words = h_raw[g][:].bitcast(F32)
+            bank = psum.tile([P, 512], F32, name="ht", tag="ht", bufs=1)
+            hT[j] = work.tile([P, 512], F32, name="hT", tag="hT")
+
+            def one(t):
+                lo = 128 * (4 * q + t)
+                nc.tensor.transpose(out=bank[:, 128 * t:128 * (t + 1)], in_=h_words[:, lo:lo + 128], identity=ident[:])
+                if t == 3:
+                    nc.scalar.copy(out=hT[j][:], in_=bank[:])
+
+            return [(one, t) for t in range(4)]
+
+        def run(steps):
+            for fn, arg in steps:
+                fn(arg)
+
+        def new_group(j):
+            a_grp[j] = work.tile([P, 4096], BF16, name="a_grp", tag="a_grp", align_bytes=64)
+
+        def quantise_a(k):
+            a_cod[k] = work.tile([P, 1024], U32, name="a_cod", tag="a_cod", align_bytes=64)
+            a_scl[k] = work.tile([P, 1024], U8, name="a_scl", tag="a_scl", align_bytes=64)
+            nc.vector.quantize_mx(out=a_cod[k][:].bitcast(FP8X4), scales=a_scl[k][:], in_=a_grp[k][:])
+
+        def regroup_msg(g, c):
+            m_grp[g, c] = work.tile([P, 1024], BF16, name="m_grp%d" % c, tag="m_grp%d" % c, bufs=1, align_bytes=64)
+            if g < V_GRAPHS:
+                nc.vector.tensor_copy(
+                    out=m_grp[g, c][:].rearrange("p (n i t) -> p n t i", n=64, i=4, t=4),
+                    in_=m_raw[g][:, 1024 * c:1024 * (c + 1)].rearrange("p (t n i) -> p n t i", t=4, n=64, i=4),
+                )
+            else:
+                src = m_raw[g][:, 1024 * c:1024 * (c + 1)].rearrange("p (t n) -> p n t", t=4)
+                dst = m_grp[g, c][:].rearrange("p (n t) -> p n t", t=4)
+                nc.gpsimd.tensor_scalar(out=dst, in0=src, scalar1=1.0, scalar2=0.0, op0=MULT, op1=ADD)
+
+        def quantise_msg(g, c):
+            m_cod[g, c] = work.tile([P, 256], U32, name="m_cod%d" % c, tag="m_cod%d" % c, align_bytes=64)
+            m_scl[g, c] = work.tile([P, 256], U8, name="m_scl%d" % c, tag="m_scl%d" % c, align_bytes=64)
+            nc.vector.quantize_mx(out=m_cod[g, c][:].bitcast(FP8X4), scales=m_scl[g, c][:], in_=m_grp[g, c][:])
+
+        def self_term(k, woven):
+            y[k] = work.tile([P, 1024], F32, name="y", tag="y", bufs=12)
+            hT_bf = hT[k][:].bitcast(BF16)
+            n = 0
+            for pair in range(2):
+                bank = psum.tile([P, 512], F32, name="acc", tag="acc", bufs=3)
+                for tt in range(2):
+                    t = 2 * pair + tt
+                    for e in range(2):
+                        if n < len(woven):
+                            run(woven[n:n + 1])
+                        n += 1
+                        nc.tensor.matmul(
+                            out=bank[:, 256 * tt:256 * (tt + 1)],
+                            lhsT=hT_bf[:, 256 * t + e:256 * (t + 1):2],
+                            rhs=wsT[:, 256 * e:256 * (e + 1)],
+                            start=(e == 0),
+                            stop=(e == 1),
+                        )
+                nc.vector.tensor_tensor(out=y[k][:, 512 * pair:512 * (pair + 1)], in0=bank[:], in1=bias2[:], op=ADD)
+
+        def aggregate(k):
+            g = k // 2
+            for pair in range(2):
+                bank = psum.tile([P, 512], F32, name="acc", tag="acc", bufs=3)
+                for tt in range(2):
+                    t = 2 * pair + tt
+                    for c in range(2):
+                        lo = 256 * t + 128 * c
+                        nc.tensor.matmul_mx(
+                            out=bank[:, 256 * tt:256 * (tt + 1)],
+                            lhsT=a_cod[k][:, lo:lo + 128].bitcast(FP8X4),
+                            lhsT_scale=a_scl[k][:, lo:lo + 128],
+                            rhs=m_cod[g, c][:].bitcast(FP8X4),
+                            rhs_scale=m_scl[g, c][:],
+                            start=(c == 0),
+                            stop=(c == 1),
+                        )
+                half = y[k][:, 512 * pair:512 * (pair + 1)]
+                nc.vector.tensor_tensor(out=half, in0=bank[:], in1=half, op=ADD)
+
+        def relu(k):
+            for pair in range(2):
+                half = y[k][:, 512 * pair:512 * (pair + 1)]
+                nc.scalar.activation(out=half, in_=half, func=RELU)
+                if k == NQ - 1:
+                    nc.sync.dma_start(out=o_view[k // 2, k % 2][:, 512 * pair:512 * (pair + 1)], in_=half)
+
+        def store(k):
+            nc.sync.dma_start(out=o_view[k // 2, k % 2], in_=y[k][:])
+
+        ident = const.tile([P, P], F32, name="ident")
+        make_identity(nc, ident[:])
+        w_raw = const.tile([P, 512], BF16, name="w_raw")
+        nc.scalar.dma_start(out=w_raw[:].rearrange("p (o c) -> p o c", o=2), in_=Ws.rearrange("(o p) c -> p o c", p=P))
+        b_row = const.tile([P, 256], BF16, name="b_row")
+        nc.vector.memset(b_row[:], 0.0)
+        nc.scalar.dma_start(out=b_row[0:1, :], in_=b.unsqueeze(0))
+        ones = const.tile([P, P], BF16, name="ones")
+        nc.vector.memset(ones[:], 1.0)
+
+        for g in range(AHEAD + 1):
+            load_graph(g)
+
+        wsT = const.tile([P, 512], BF16, name="wsT")
+        bias2 = const.tile([P, 512], F32, name="bias2")
+        w_words = w_raw[:].bitcast(F32)
+        w_bank = psum.tile([P, 512], F32, name="ht", tag="ht", bufs=1)
+        for o in range(2):
+            nc.tensor.transpose(out=w_bank[:, 128 * o:128 * (o + 1)], in_=w_words[:, 128 * o:128 * (o + 1)], identity=ident[:])
+        nc.vector.tensor_copy(
+            out=wsT[:].rearrange("p (e o) -> p e o", e=2),
+            in_=w_bank[:, 0:256].bitcast(BF16).rearrange("p (o e) -> p e o", e=2),
+        )
+        b_bank = psum.tile([P, 512], F32, name="acc", tag="acc", bufs=3)
+        nc.tensor.matmul(out=b_bank[:, 0:256], lhsT=ones[:], rhs=b_row[:], start=True, stop=True)
+        for r in range(2):
+            nc.vector.tensor_copy(out=bias2[:, 256 * r:256 * (r + 1)], in_=b_bank[:, 0:256])
+
+        def stores_by(j):
+            lag = ST_LAG if j <= 2 * (G - 1 - AHEAD) else 2
+            return max(0, min(j - lag + 1, NQ - 1))
+
+        for j in range(NQ + 2):
+            k = j - 1
+            if j >= 2 and j % 2 == 0 and j // 2 + AHEAD < G:
+                load_graph(j // 2 + AHEAD)
+            if j >= 2:
+                relu(j - 2)
+            for kk in range(stores_by(j - 1), stores_by(j)):
+                store(kk)
+            woven = []
+            if j < NQ:
+                new_group(j)
+                bunched = 3 if (WEAVE and j >= 2) else 4
+                for t in range(bunched):
+                    run(a_tile_steps(j, t))
+                if bunched == 3:
+                    woven = a_tile_steps(j, 3) + h_steps(j)
+                else:
+                    run(h_steps(j))
+            if j == 0:
+                quantise_a(0)
+                regroup_msg(0, 0)
+                regroup_msg(0, 1)
+                quantise_msg(0, 0)
+                quantise_msg(0, 1)
+                self_term(0, [])
+                aggregate(0)
+            if 2 <= j <= NQ:
+                quantise_a(k)
+                if k == 1:
+                    regroup_msg(1, 0)
+                    regroup_msg(1, 1)
+                g, c = divmod(k + 1, 2)
+                if g < G:
+                    quantise_msg(g, c)
+                    if V_GRAPHS <= g + 1 < G:
+                        regroup_msg(g + 1, c)
+                self_term(k, woven)
+                aggregate(k)

@@ -12,7 +12,9 @@ U8 = mybir.dt.uint8
 FP8X4 = mybir.dt.float8_e4m3fn_x4
 ADD = mybir.AluOpType.add
 MULT = mybir.AluOpType.mult
-RELU = mybir.ActivationFunctionType.Relu
+MIN = mybir.AluOpType.min
+MAX = mybir.AluOpType.max
+F32_MAX = (2.0 - 2.0**-23) * 2.0**127
 P = 128
 AHEAD = 3
 ST_LAG = 4
@@ -170,7 +172,7 @@ def tile_gcnstacking_pb_t_kernel(tc, A, msg, h, Ws, b, out):
         def relu(k):
             for pair in range(2):
                 half = y[k][:, 512 * pair:512 * (pair + 1)]
-                nc.scalar.activation(out=half, in_=half, func=RELU)
+                nc.gpsimd.tensor_scalar(out=half, in0=half, scalar1=F32_MAX, scalar2=0.0, op0=MIN, op1=MAX)
                 if k == NQ - 1:
                     nc.sync.dma_start(out=o_view[k // 2, k % 2][:, 512 * pair:512 * (pair + 1)], in_=half)
 

@@ -12,14 +12,15 @@ U8 = mybir.dt.uint8
 FP8X4 = mybir.dt.float8_e4m3fn_x4
 ADD = mybir.AluOpType.add
 MULT = mybir.AluOpType.mult
+RELU = mybir.ActivationFunctionType.Relu
 MIN = mybir.AluOpType.min
 MAX = mybir.AluOpType.max
 F32_MAX = (2.0 - 2.0**-23) * 2.0**127
 P = 128
 AHEAD = 3
 ST_LAG = 4
-WEAVE = True
-V_GRAPHS = 2
+PERM = 1
+GP_HALVES = 1
 
 
 def tile_gcnstacking_pb_t_kernel(tc, A, msg, h, Ws, b, out):
@@ -40,6 +41,7 @@ def tile_gcnstacking_pb_t_kernel(tc, A, msg, h, Ws, b, out):
         ctx.enter_context(tc.manual_schedule())
 
         a_raw, h_raw, m_raw = {}, {}, {}
+        a_per = {}
         a_grp, a_cod, a_scl = {}, {}, {}
         m_grp, m_cod, m_scl = {}, {}, {}
         hT, y = {}, {}
@@ -48,35 +50,44 @@ def tile_gcnstacking_pb_t_kernel(tc, A, msg, h, Ws, b, out):
             m_raw[g] = raw.tile([P, 2048], BF16, name="m_raw", tag="m_raw", bufs=AHEAD + 2)
             nc.sync.dma_start(out=m_raw[g][:].rearrange("p (c x) -> p c x", c=2), in_=m_view[g])
 
-        def load_graph(g):
-            a_raw[2 * g] = raw.tile([P, 4096], BF16, name="a_raw", tag="a_raw", bufs=2 * (AHEAD + 1))
+        def load_h(g):
             h_raw[g] = raw.tile([P, 2048], BF16, name="h_raw", tag="h_raw", bufs=AHEAD + 1)
-            a_raw[2 * g + 1] = raw.tile([P, 4096], BF16, name="a_raw", tag="a_raw", bufs=2 * (AHEAD + 1))
+            nc.sync.dma_start(out=h_raw[g][:], in_=h_view[g])
+
+        def load_a(j, pieces):
+            a_raw[j] = raw.tile([P, 4096], BF16, name="a_raw", tag="a_raw", bufs=2 * (AHEAD + 1))
+            w = 4096 // pieces
+            for i in range(pieces):
+                nc.sync.dma_start(out=a_raw[j][:, w * i:w * (i + 1)], in_=a_view[j // 2, j % 2][:, w * i:w * (i + 1)])
+
+        def load_graph(g):
             if g == 0:
-                for t in range(4):
-                    nc.sync.dma_start(out=a_raw[0][:, 1024 * t:1024 * (t + 1)], in_=a_view[0, 0][:, 1024 * t:1024 * (t + 1)])
-                nc.sync.dma_start(out=h_raw[g][:], in_=h_view[g])
+                load_a(0, 4)
                 load_msg(0)
+                load_h(0)
+                load_a(1, 4)
             else:
-                if g == 2:
-                    load_msg(2)
-                nc.sync.dma_start(out=a_raw[2 * g][:], in_=a_view[g, 0])
                 if g == 1:
                     load_msg(1)
-                elif g + 1 < G:
+                load_a(2 * g, 1)
+                load_h(g)
+                if g + 1 < G:
                     load_msg(g + 1)
-                nc.sync.dma_start(out=h_raw[g][:], in_=h_view[g])
-            nc.sync.dma_start(out=a_raw[2 * g + 1][:], in_=a_view[g, 1])
+                load_a(2 * g + 1, 1)
 
         def a_tile_steps(j, t):
-            words = a_raw[j][:].bitcast(F32)
+            if (j, t) in a_per:
+                words, base, step = a_per[j, t][:], 0, 1
+            else:
+                words, base, step = a_raw[j][:].bitcast(F32), 512 * t, 2
             grp_words = a_grp[j][:].bitcast(F32)
             bank = psum.tile([P, 512], F32, name="at", tag="at", bufs=4)
 
             def one(s):
                 c, u = divmod(s, 2)
-                lo = 512 * t + 256 * c
-                nc.tensor.transpose(out=bank[:, 128 * s:128 * (s + 1)], in_=words[:, lo + u:lo + 256:2], identity=ident[:])
+                lo = base + 256 * c
+                cols = slice(lo + u, lo + 256, 2) if step == 2 else slice(lo + 128 * u, lo + 128 * (u + 1))
+                nc.tensor.transpose(out=bank[:, 128 * s:128 * (s + 1)], in_=words[:, cols], identity=ident[:])
                 if s == 3:
                     nc.scalar.copy(
                         out=grp_words[:, 512 * t:512 * (t + 1)].rearrange("p (c i u) -> p c i u", c=2, i=128, u=2),
@@ -84,6 +95,13 @@ def tile_gcnstacking_pb_t_kernel(tc, A, msg, h, Ws, b, out):
                     )
 
             return [(one, s) for s in range(4)]
+
+        def permute(j, t):
+            a_per[j, t] = work.tile([P, 512], F32, name="a_per", tag="a_per", bufs=2 * PERM)
+            nc.scalar.copy(
+                out=a_per[j, t][:].rearrange("p (c u w) -> p c u w", c=2, u=2),
+                in_=a_raw[j][:].bitcast(F32)[:, 512 * t:512 * (t + 1)].rearrange("p (c w u) -> p c u w", c=2, u=2),
+            )
 
         def h_steps(j):
             g, q = divmod(j, 2)
@@ -113,7 +131,7 @@ def tile_gcnstacking_pb_t_kernel(tc, A, msg, h, Ws, b, out):
 
         def regroup_msg(g, c):
             m_grp[g, c] = work.tile([P, 1024], BF16, name="m_grp%d" % c, tag="m_grp%d" % c, bufs=1, align_bytes=64)
-            if g < V_GRAPHS:
+            if g == 0:
                 nc.vector.tensor_copy(
                     out=m_grp[g, c][:].rearrange("p (n i t) -> p n t i", n=64, i=4, t=4),
                     in_=m_raw[g][:, 1024 * c:1024 * (c + 1)].rearrange("p (t n i) -> p n t i", t=4, n=64, i=4),
@@ -169,12 +187,14 @@ def tile_gcnstacking_pb_t_kernel(tc, A, msg, h, Ws, b, out):
                 half = y[k][:, 512 * pair:512 * (pair + 1)]
                 nc.vector.tensor_tensor(out=half, in0=bank[:], in1=half, op=ADD)
 
-        def relu(k):
-            for pair in range(2):
-                half = y[k][:, 512 * pair:512 * (pair + 1)]
+        def relu(k, pair):
+            half = y[k][:, 512 * pair:512 * (pair + 1)]
+            if pair >= 2 - GP_HALVES and k < NQ - 2:
                 nc.gpsimd.tensor_scalar(out=half, in0=half, scalar1=F32_MAX, scalar2=0.0, op0=MIN, op1=MAX)
-                if k == NQ - 1:
-                    nc.sync.dma_start(out=o_view[k // 2, k % 2][:, 512 * pair:512 * (pair + 1)], in_=half)
+            else:
+                nc.scalar.activation(out=half, in_=half, func=RELU)
+            if k == NQ - 1:
+                nc.sync.dma_start(out=o_view[k // 2, k % 2][:, 512 * pair:512 * (pair + 1)], in_=half)
 
         def store(k):
             nc.sync.dma_start(out=o_view[k // 2, k % 2], in_=y[k][:])
@@ -194,18 +214,20 @@ def tile_gcnstacking_pb_t_kernel(tc, A, msg, h, Ws, b, out):
 
         wsT = const.tile([P, 512], BF16, name="wsT")
         bias2 = const.tile([P, 512], F32, name="bias2")
-        w_words = w_raw[:].bitcast(F32)
-        w_bank = psum.tile([P, 512], F32, name="ht", tag="ht", bufs=1)
-        for o in range(2):
-            nc.tensor.transpose(out=w_bank[:, 128 * o:128 * (o + 1)], in_=w_words[:, 128 * o:128 * (o + 1)], identity=ident[:])
-        nc.vector.tensor_copy(
-            out=wsT[:].rearrange("p (e o) -> p e o", e=2),
-            in_=w_bank[:, 0:256].bitcast(BF16).rearrange("p (o e) -> p e o", e=2),
-        )
-        b_bank = psum.tile([P, 512], F32, name="acc", tag="acc", bufs=3)
-        nc.tensor.matmul(out=b_bank[:, 0:256], lhsT=ones[:], rhs=b_row[:], start=True, stop=True)
-        for r in range(2):
-            nc.vector.tensor_copy(out=bias2[:, 256 * r:256 * (r + 1)], in_=b_bank[:, 0:256])
+
+        def make_weights():
+            w_words = w_raw[:].bitcast(F32)
+            w_bank = psum.tile([P, 512], F32, name="ht", tag="ht", bufs=1)
+            for o in range(2):
+                nc.tensor.transpose(out=w_bank[:, 128 * o:128 * (o + 1)], in_=w_words[:, 128 * o:128 * (o + 1)], identity=ident[:])
+            nc.vector.tensor_copy(
+                out=wsT[:].rearrange("p (e o) -> p e o", e=2),
+                in_=w_bank[:, 0:256].bitcast(BF16).rearrange("p (o e) -> p e o", e=2),
+            )
+            b_bank = psum.tile([P, 512], F32, name="acc", tag="acc", bufs=3)
+            nc.tensor.matmul(out=b_bank[:, 0:256], lhsT=ones[:], rhs=b_row[:], start=True, stop=True)
+            for r in range(2):
+                nc.vector.tensor_copy(out=bias2[:, 256 * r:256 * (r + 1)], in_=b_bank[:, 0:256])
 
         def stores_by(j):
             lag = ST_LAG if j <= 2 * (G - 1 - AHEAD) else 2
@@ -216,36 +238,42 @@ def tile_gcnstacking_pb_t_kernel(tc, A, msg, h, Ws, b, out):
             if j >= 2 and j % 2 == 0 and j // 2 + AHEAD < G:
                 load_graph(j // 2 + AHEAD)
             if j >= 2:
-                relu(j - 2)
-            for kk in range(stores_by(j - 1), stores_by(j)):
-                store(kk)
+                relu(j - 2, 0)
             woven = []
             if j < NQ:
                 new_group(j)
-                bunched = 3 if (WEAVE and j >= 2) else 4
+                bunched = 4 - PERM if j >= 2 else 4
                 for t in range(bunched):
                     run(a_tile_steps(j, t))
-                if bunched == 3:
-                    woven = a_tile_steps(j, 3) + h_steps(j)
+                    if j == 0 and t == 0:
+                        make_weights()
+                    if 2 <= j + 1 < NQ and t >= bunched - PERM:
+                        permute(j + 1, t - bunched + 4)
+                for t in range(bunched, 4):
+                    woven += a_tile_steps(j, t)
+                if j >= 1 and len(woven) <= 4:
+                    woven += h_steps(j)
                 else:
                     run(h_steps(j))
-            if j == 0:
-                quantise_a(0)
-                regroup_msg(0, 0)
-                regroup_msg(0, 1)
-                quantise_msg(0, 0)
-                quantise_msg(0, 1)
-                self_term(0, [])
-                aggregate(0)
-            if 2 <= j <= NQ:
+            if 1 <= j <= NQ:
                 quantise_a(k)
-                if k == 1:
-                    regroup_msg(1, 0)
-                    regroup_msg(1, 1)
-                g, c = divmod(k + 1, 2)
-                if g < G:
-                    quantise_msg(g, c)
-                    if V_GRAPHS <= g + 1 < G:
-                        regroup_msg(g + 1, c)
+                if j == 1:
+                    for c in range(2):
+                        regroup_msg(0, c)
+                    for c in range(2):
+                        quantise_msg(0, c)
+                    for c in range(2):
+                        regroup_msg(1, c)
+                else:
+                    g, c = divmod(k + 1, 2)
+                    if g < G:
+                        quantise_msg(g, c)
+                        if g + 1 < G:
+                            regroup_msg(g + 1, c)
+            if j >= 2:
+                relu(j - 2, 1)
+                for kk in range(stores_by(j - 1), stores_by(j)):
+                    store(kk)
+            if 1 <= j <= NQ:
                 self_term(k, woven)
                 aggregate(k)

@@ -19,8 +19,10 @@ F32_MAX = (2.0 - 2.0**-23) * 2.0**127
 P = 128
 AHEAD = 3
 ST_LAG = 4
-PERM = 1
-GP_HALVES = 1
+PERM = 2
+FIRST_PERM = 4
+GP_LAST = 11
+VECTOR_TILES = [(0, 1), (0, 3)]
 
 
 def tile_gcnstacking_pb_t_kernel(tc, A, msg, h, Ws, b, out):
@@ -63,9 +65,9 @@ def tile_gcnstacking_pb_t_kernel(tc, A, msg, h, Ws, b, out):
         def load_graph(g):
             if g == 0:
                 load_a(0, 4)
-                load_msg(0)
                 load_h(0)
                 load_a(1, 4)
+                load_msg(0)
             else:
                 if g == 1:
                     load_msg(1)
@@ -89,7 +91,8 @@ def tile_gcnstacking_pb_t_kernel(tc, A, msg, h, Ws, b, out):
                 cols = slice(lo + u, lo + 256, 2) if step == 2 else slice(lo + 128 * u, lo + 128 * (u + 1))
                 nc.tensor.transpose(out=bank[:, 128 * s:128 * (s + 1)], in_=words[:, cols], identity=ident[:])
                 if s == 3:
-                    nc.scalar.copy(
+                    copy = nc.vector.tensor_copy if (j, t) in VECTOR_TILES else nc.scalar.copy
+                    copy(
                         out=grp_words[:, 512 * t:512 * (t + 1)].rearrange("p (c i u) -> p c i u", c=2, i=128, u=2),
                         in_=bank[:].rearrange("p (c u i) -> p c i u", c=2, u=2, i=128),
                     )
@@ -106,7 +109,10 @@ def tile_gcnstacking_pb_t_kernel(tc, A, msg, h, Ws, b, out):
         def h_steps(j):
             g, q = divmod(j, 2)
             h_words = h_raw[g][:].bitcast(F32)
-            bank = psum.tile([P, 512], F32, name="ht", tag="ht", bufs=1)
+            if j == 1:
+                bank = psum.tile([P, 512], F32, name="acc", tag="acc", bufs=3)
+            else:
+                bank = psum.tile([P, 512], F32, name="ht", tag="ht", bufs=1)
             hT[j] = work.tile([P, 512], F32, name="hT", tag="hT")
 
             def one(t):
@@ -127,7 +133,11 @@ def tile_gcnstacking_pb_t_kernel(tc, A, msg, h, Ws, b, out):
         def quantise_a(k):
             a_cod[k] = work.tile([P, 1024], U32, name="a_cod", tag="a_cod", align_bytes=64)
             a_scl[k] = work.tile([P, 1024], U8, name="a_scl", tag="a_scl", align_bytes=64)
-            nc.vector.quantize_mx(out=a_cod[k][:].bitcast(FP8X4), scales=a_scl[k][:], in_=a_grp[k][:])
+            for lo in range(0, 1024, 512 if k == NQ - 1 else 1024):
+                cols = slice(lo, lo + (512 if k == NQ - 1 else 1024))
+                nc.vector.quantize_mx(
+                    out=a_cod[k][:, cols].bitcast(FP8X4), scales=a_scl[k][:, cols], in_=a_grp[k][:, 4 * cols.start:4 * cols.stop]
+                )
 
         def regroup_msg(g, c):
             m_grp[g, c] = work.tile([P, 1024], BF16, name="m_grp%d" % c, tag="m_grp%d" % c, bufs=1, align_bytes=64)
@@ -154,6 +164,8 @@ def tile_gcnstacking_pb_t_kernel(tc, A, msg, h, Ws, b, out):
                 bank = psum.tile([P, 512], F32, name="acc", tag="acc", bufs=3)
                 for tt in range(2):
                     t = 2 * pair + tt
+                    if k == NQ - 1:
+                        nc.tensor.matmul(out=bank[:, 256 * tt:256 * (tt + 1)], lhsT=ones[:], rhs=b_row[:], start=True, stop=False)
                     for e in range(2):
                         if n < len(woven):
                             run(woven[n:n + 1])
@@ -162,10 +174,14 @@ def tile_gcnstacking_pb_t_kernel(tc, A, msg, h, Ws, b, out):
                             out=bank[:, 256 * tt:256 * (tt + 1)],
                             lhsT=hT_bf[:, 256 * t + e:256 * (t + 1):2],
                             rhs=wsT[:, 256 * e:256 * (e + 1)],
-                            start=(e == 0),
+                            start=(e == 0 and k < NQ - 1),
                             stop=(e == 1),
                         )
-                nc.vector.tensor_tensor(out=y[k][:, 512 * pair:512 * (pair + 1)], in0=bank[:], in1=bias2[:], op=ADD)
+                half = y[k][:, 512 * pair:512 * (pair + 1)]
+                if k == NQ - 1:
+                    nc.scalar.copy(out=half, in_=bank[:])
+                else:
+                    nc.vector.tensor_tensor(out=half, in0=bank[:], in1=bias2[:], op=ADD)
 
         def aggregate(k):
             g = k // 2
@@ -189,7 +205,7 @@ def tile_gcnstacking_pb_t_kernel(tc, A, msg, h, Ws, b, out):
 
         def relu(k, pair):
             half = y[k][:, 512 * pair:512 * (pair + 1)]
-            if pair >= 2 - GP_HALVES and k < NQ - 2:
+            if (pair == 1 or k % 2 == 0) and k <= GP_LAST:
                 nc.gpsimd.tensor_scalar(out=half, in0=half, scalar1=F32_MAX, scalar2=0.0, op0=MIN, op1=MAX)
             else:
                 nc.scalar.activation(out=half, in_=half, func=RELU)
@@ -224,6 +240,8 @@ def tile_gcnstacking_pb_t_kernel(tc, A, msg, h, Ws, b, out):
                 out=wsT[:].rearrange("p (e o) -> p e o", e=2),
                 in_=w_bank[:, 0:256].bitcast(BF16).rearrange("p (o e) -> p e o", e=2),
             )
+
+        def make_bias():
             b_bank = psum.tile([P, 512], F32, name="acc", tag="acc", bufs=3)
             nc.tensor.matmul(out=b_bank[:, 0:256], lhsT=ones[:], rhs=b_row[:], start=True, stop=True)
             for r in range(2):
@@ -233,47 +251,55 @@ def tile_gcnstacking_pb_t_kernel(tc, A, msg, h, Ws, b, out):
             lag = ST_LAG if j <= 2 * (G - 1 - AHEAD) else 2
             return max(0, min(j - lag + 1, NQ - 1))
 
-        for j in range(NQ + 2):
+        new_group(0)
+        for t in range(4):
+            run(a_tile_steps(0, t))
+        make_weights()
+        quantise_a(0)
+        for j in range(2):
+            run(h_steps(j))
+        new_group(1)
+        for t in range(4):
+            run(a_tile_steps(1, t))
+        make_bias()
+        for c in range(2):
+            regroup_msg(0, c)
+        for c in range(2):
+            quantise_msg(0, c)
+        for c in range(2):
+            regroup_msg(1, c)
+        self_term(0, [])
+        aggregate(0)
+
+        for j in range(2, NQ + 2):
             k = j - 1
-            if j >= 2 and j % 2 == 0 and j // 2 + AHEAD < G:
+            if j % 2 == 0 and j // 2 + AHEAD < G:
                 load_graph(j // 2 + AHEAD)
-            if j >= 2:
-                relu(j - 2, 0)
+            relu(j - 2, 0)
             woven = []
             if j < NQ:
                 new_group(j)
-                bunched = 4 - PERM if j >= 2 else 4
+                bunched = 4 - PERM
                 for t in range(bunched):
                     run(a_tile_steps(j, t))
-                    if j == 0 and t == 0:
-                        make_weights()
-                    if 2 <= j + 1 < NQ and t >= bunched - PERM:
+                    if FIRST_PERM <= j + 1 < NQ and t >= bunched - PERM:
                         permute(j + 1, t - bunched + 4)
                 for t in range(bunched, 4):
                     woven += a_tile_steps(j, t)
-                if j >= 1 and len(woven) <= 4:
+                if len(woven) <= 4:
                     woven += h_steps(j)
                 else:
                     run(h_steps(j))
-            if 1 <= j <= NQ:
+            if j <= NQ:
                 quantise_a(k)
-                if j == 1:
-                    for c in range(2):
-                        regroup_msg(0, c)
-                    for c in range(2):
-                        quantise_msg(0, c)
-                    for c in range(2):
-                        regroup_msg(1, c)
-                else:
-                    g, c = divmod(k + 1, 2)
-                    if g < G:
-                        quantise_msg(g, c)
-                        if g + 1 < G:
-                            regroup_msg(g + 1, c)
-            if j >= 2:
-                relu(j - 2, 1)
-                for kk in range(stores_by(j - 1), stores_by(j)):
-                    store(kk)
-            if 1 <= j <= NQ:
+                g, c = divmod(k + 1, 2)
+                if g < G:
+                    quantise_msg(g, c)
+                    if g + 1 < G:
+                        regroup_msg(g + 1, c)
+            relu(j - 2, 1)
+            for kk in range(stores_by(j - 1), stores_by(j)):
+                store(kk)
+            if j <= NQ:
                 self_term(k, woven)
                 aggregate(k)

@@ -20,8 +20,9 @@ P = 128
 AHEAD = 3
 ST_LAG = 4
 PERM = 2
-FIRST_PERM = 4
-GP_LAST = 11
+GP_PERM = 1
+FIRST_PERM = 3
+GP_LAST = 13
 VECTOR_TILES = [(0, 1), (0, 3)]
 
 
@@ -70,26 +71,28 @@ def tile_gcnstacking_pb_t_kernel(tc, A, msg, h, Ws, b, out):
                 load_msg(0)
             else:
                 if g == 1:
+                    load_a(2, 1)
+                    load_h(1)
                     load_msg(1)
-                load_a(2 * g, 1)
-                load_h(g)
-                if g + 1 < G:
-                    load_msg(g + 1)
+                else:
+                    load_msg(g)
+                    load_a(2 * g, 1)
+                    load_h(g)
                 load_a(2 * g + 1, 1)
 
         def a_tile_steps(j, t):
-            if (j, t) in a_per:
-                words, base, step = a_per[j, t][:], 0, 1
-            else:
-                words, base, step = a_raw[j][:].bitcast(F32), 512 * t, 2
             grp_words = a_grp[j][:].bitcast(F32)
             bank = psum.tile([P, 512], F32, name="at", tag="at", bufs=4)
 
             def one(s):
                 c, u = divmod(s, 2)
-                lo = base + 256 * c
-                cols = slice(lo + u, lo + 256, 2) if step == 2 else slice(lo + 128 * u, lo + 128 * (u + 1))
-                nc.tensor.transpose(out=bank[:, 128 * s:128 * (s + 1)], in_=words[:, cols], identity=ident[:])
+                if (j, t) in a_per:
+                    lo = 256 * u + 128 * c
+                    words = a_per[j, t][:, lo:lo + 128]
+                else:
+                    lo = 512 * t + 256 * c
+                    words = a_raw[j][:].bitcast(F32)[:, lo + u:lo + 256:2]
+                nc.tensor.transpose(out=bank[:, 128 * s:128 * (s + 1)], in_=words, identity=ident[:])
                 if s == 3:
                     copy = nc.vector.tensor_copy if (j, t) in VECTOR_TILES else nc.scalar.copy
                     copy(
@@ -101,10 +104,20 @@ def tile_gcnstacking_pb_t_kernel(tc, A, msg, h, Ws, b, out):
 
         def permute(j, t):
             a_per[j, t] = work.tile([P, 512], F32, name="a_per", tag="a_per", bufs=2 * PERM)
-            nc.scalar.copy(
-                out=a_per[j, t][:].rearrange("p (c u w) -> p c u w", c=2, u=2),
-                in_=a_raw[j][:].bitcast(F32)[:, 512 * t:512 * (t + 1)].rearrange("p (c w u) -> p c u w", c=2, u=2),
-            )
+            if t >= 4 - GP_PERM:
+                nc.gpsimd.tensor_scalar(
+                    out=a_per[j, t][:].bitcast(BF16).rearrange("p (u w e) -> p u w e", u=2, e=2),
+                    in0=a_raw[j][:, 1024 * t:1024 * (t + 1)].rearrange("p (w u e) -> p u w e", u=2, e=2),
+                    scalar1=1.0,
+                    scalar2=0.0,
+                    op0=MULT,
+                    op1=ADD,
+                )
+            else:
+                nc.scalar.copy(
+                    out=a_per[j, t][:].rearrange("p (u w) -> p u w", u=2),
+                    in_=a_raw[j][:].bitcast(F32)[:, 512 * t:512 * (t + 1)].rearrange("p (w u) -> p u w", u=2),
+                )
 
         def h_steps(j):
             g, q = divmod(j, 2)
@@ -203,14 +216,15 @@ def tile_gcnstacking_pb_t_kernel(tc, A, msg, h, Ws, b, out):
                 half = y[k][:, 512 * pair:512 * (pair + 1)]
                 nc.vector.tensor_tensor(out=half, in0=bank[:], in1=half, op=ADD)
 
-        def relu(k, pair):
-            half = y[k][:, 512 * pair:512 * (pair + 1)]
-            if (pair == 1 or k % 2 == 0) and k <= GP_LAST:
-                nc.gpsimd.tensor_scalar(out=half, in0=half, scalar1=F32_MAX, scalar2=0.0, op0=MIN, op1=MAX)
-            else:
+        def relu(k):
+            if k <= GP_LAST:
+                nc.gpsimd.tensor_scalar(out=y[k][:], in0=y[k][:], scalar1=F32_MAX, scalar2=0.0, op0=MIN, op1=MAX)
+                return
+            for pair in range(2):
+                half = y[k][:, 512 * pair:512 * (pair + 1)]
                 nc.scalar.activation(out=half, in_=half, func=RELU)
-            if k == NQ - 1:
-                nc.sync.dma_start(out=o_view[k // 2, k % 2][:, 512 * pair:512 * (pair + 1)], in_=half)
+                if k == NQ - 1:
+                    nc.sync.dma_start(out=o_view[k // 2, k % 2][:, 512 * pair:512 * (pair + 1)], in_=half)
 
         def store(k):
             nc.sync.dma_start(out=o_view[k // 2, k % 2], in_=y[k][:])
@@ -261,13 +275,12 @@ def tile_gcnstacking_pb_t_kernel(tc, A, msg, h, Ws, b, out):
         new_group(1)
         for t in range(4):
             run(a_tile_steps(1, t))
-        make_bias()
         for c in range(2):
             regroup_msg(0, c)
         for c in range(2):
             quantise_msg(0, c)
-        for c in range(2):
-            regroup_msg(1, c)
+        make_bias()
+        regroup_msg(1, 0)
         self_term(0, [])
         aggregate(0)
 
@@ -275,31 +288,27 @@ def tile_gcnstacking_pb_t_kernel(tc, A, msg, h, Ws, b, out):
             k = j - 1
             if j % 2 == 0 and j // 2 + AHEAD < G:
                 load_graph(j // 2 + AHEAD)
-            relu(j - 2, 0)
+            relu(j - 2)
+            for kk in range(stores_by(j - 1), stores_by(j)):
+                store(kk)
             woven = []
             if j < NQ:
                 new_group(j)
-                bunched = 4 - PERM
-                for t in range(bunched):
+                for t in range(2):
                     run(a_tile_steps(j, t))
-                    if FIRST_PERM <= j + 1 < NQ and t >= bunched - PERM:
-                        permute(j + 1, t - bunched + 4)
-                for t in range(bunched, 4):
+                    if t == 0 and FIRST_PERM <= j + 1 < NQ:
+                        for tt in range(4 - PERM, 4):
+                            permute(j + 1, tt)
+                run(h_steps(j))
+                for t in range(2, 4):
                     woven += a_tile_steps(j, t)
-                if len(woven) <= 4:
-                    woven += h_steps(j)
-                else:
-                    run(h_steps(j))
             if j <= NQ:
                 quantise_a(k)
                 g, c = divmod(k + 1, 2)
                 if g < G:
                     quantise_msg(g, c)
-                    if g + 1 < G:
-                        regroup_msg(g + 1, c)
-            relu(j - 2, 1)
-            for kk in range(stores_by(j - 1), stores_by(j)):
-                store(kk)
-            if j <= NQ:
+                g, c = divmod(k + 2, 2)
+                if g < G:
+                    regroup_msg(g, c)
                 self_term(k, woven)
                 aggregate(k)

@@ -20,10 +20,18 @@ P = 128
 AHEAD = 3
 ST_LAG = 4
 PERM = 2
-GP_PERM = 1
-FIRST_PERM = 3
-GP_LAST = 13
+FIRST_PERM = 4
 VECTOR_TILES = [(0, 1), (0, 3)]
+
+
+def relu_engine(k, pair):
+    if k >= 14:
+        return ("gpsimd", "vector", "scalar", "vector")[2 * (k - 14) + pair]
+    return ("vector", "gpsimd")[pair]
+
+
+def perms(j):
+    return 0 if j < FIRST_PERM else PERM
 
 
 def tile_gcnstacking_pb_t_kernel(tc, A, msg, h, Ws, b, out):
@@ -70,14 +78,9 @@ def tile_gcnstacking_pb_t_kernel(tc, A, msg, h, Ws, b, out):
                 load_a(1, 4)
                 load_msg(0)
             else:
-                if g == 1:
-                    load_a(2, 1)
-                    load_h(1)
-                    load_msg(1)
-                else:
-                    load_msg(g)
-                    load_a(2 * g, 1)
-                    load_h(g)
+                load_msg(g)
+                load_a(2 * g, 1)
+                load_h(g)
                 load_a(2 * g + 1, 1)
 
         def a_tile_steps(j, t):
@@ -104,20 +107,10 @@ def tile_gcnstacking_pb_t_kernel(tc, A, msg, h, Ws, b, out):
 
         def permute(j, t):
             a_per[j, t] = work.tile([P, 512], F32, name="a_per", tag="a_per", bufs=2 * PERM)
-            if t >= 4 - GP_PERM:
-                nc.gpsimd.tensor_scalar(
-                    out=a_per[j, t][:].bitcast(BF16).rearrange("p (u w e) -> p u w e", u=2, e=2),
-                    in0=a_raw[j][:, 1024 * t:1024 * (t + 1)].rearrange("p (w u e) -> p u w e", u=2, e=2),
-                    scalar1=1.0,
-                    scalar2=0.0,
-                    op0=MULT,
-                    op1=ADD,
-                )
-            else:
-                nc.scalar.copy(
-                    out=a_per[j, t][:].rearrange("p (u w) -> p u w", u=2),
-                    in_=a_raw[j][:].bitcast(F32)[:, 512 * t:512 * (t + 1)].rearrange("p (w u) -> p u w", u=2),
-                )
+            nc.scalar.copy(
+                out=a_per[j, t][:].rearrange("p (u w) -> p u w", u=2),
+                in_=a_raw[j][:].bitcast(F32)[:, 512 * t:512 * (t + 1)].rearrange("p (w u) -> p u w", u=2),
+            )
 
         def h_steps(j):
             g, q = divmod(j, 2)
@@ -174,7 +167,10 @@ def tile_gcnstacking_pb_t_kernel(tc, A, msg, h, Ws, b, out):
             hT_bf = hT[k][:].bitcast(BF16)
             n = 0
             for pair in range(2):
-                bank = psum.tile([P, 512], F32, name="acc", tag="acc", bufs=3)
+                if k == NQ - 1:
+                    bank = psum.tile([P, 512], F32, name="at", tag="at", bufs=4)
+                else:
+                    bank = psum.tile([P, 512], F32, name="acc", tag="acc", bufs=3)
                 for tt in range(2):
                     t = 2 * pair + tt
                     if k == NQ - 1:
@@ -216,14 +212,18 @@ def tile_gcnstacking_pb_t_kernel(tc, A, msg, h, Ws, b, out):
                 half = y[k][:, 512 * pair:512 * (pair + 1)]
                 nc.vector.tensor_tensor(out=half, in0=bank[:], in1=half, op=ADD)
 
-        def relu(k):
-            if k <= GP_LAST:
-                nc.gpsimd.tensor_scalar(out=y[k][:], in0=y[k][:], scalar1=F32_MAX, scalar2=0.0, op0=MIN, op1=MAX)
-                return
+        def relu(k, engine):
             for pair in range(2):
+                if relu_engine(k, pair) != engine:
+                    continue
                 half = y[k][:, 512 * pair:512 * (pair + 1)]
-                nc.scalar.activation(out=half, in_=half, func=RELU)
-                if k == NQ - 1:
+                if engine == "scalar":
+                    nc.scalar.activation(out=half, in_=half, func=RELU)
+                elif engine == "vector":
+                    nc.vector.tensor_scalar(out=half, in0=half, scalar1=0.0, scalar2=None, op0=MAX)
+                else:
+                    nc.gpsimd.tensor_scalar(out=half, in0=half, scalar1=F32_MAX, scalar2=0.0, op0=MIN, op1=MAX)
+                if k >= NQ - 2:
                     nc.sync.dma_start(out=o_view[k // 2, k % 2][:, 512 * pair:512 * (pair + 1)], in_=half)
 
         def store(k):
@@ -263,7 +263,7 @@ def tile_gcnstacking_pb_t_kernel(tc, A, msg, h, Ws, b, out):
 
         def stores_by(j):
             lag = ST_LAG if j <= 2 * (G - 1 - AHEAD) else 2
-            return max(0, min(j - lag + 1, NQ - 1))
+            return max(0, min(j - lag + 1, NQ - 2))
 
         new_group(0)
         for t in range(4):
@@ -280,7 +280,8 @@ def tile_gcnstacking_pb_t_kernel(tc, A, msg, h, Ws, b, out):
         for c in range(2):
             quantise_msg(0, c)
         make_bias()
-        regroup_msg(1, 0)
+        for c in range(2):
+            regroup_msg(1, c)
         self_term(0, [])
         aggregate(0)
 
@@ -288,27 +289,37 @@ def tile_gcnstacking_pb_t_kernel(tc, A, msg, h, Ws, b, out):
             k = j - 1
             if j % 2 == 0 and j // 2 + AHEAD < G:
                 load_graph(j // 2 + AHEAD)
-            relu(j - 2)
-            for kk in range(stores_by(j - 1), stores_by(j)):
-                store(kk)
             woven = []
             if j < NQ:
                 new_group(j)
+                if j > 2:
+                    run(h_steps(j))
                 for t in range(2):
                     run(a_tile_steps(j, t))
-                    if t == 0 and FIRST_PERM <= j + 1 < NQ:
-                        for tt in range(4 - PERM, 4):
-                            permute(j + 1, tt)
-                run(h_steps(j))
+                if j == 2:
+                    run(h_steps(j))
+                if FIRST_PERM <= j + 1 < NQ:
+                    for tt in range(4 - perms(j + 1), 4):
+                        permute(j + 1, tt)
                 for t in range(2, 4):
                     woven += a_tile_steps(j, t)
-            if j <= NQ:
+            if j < NQ:
                 quantise_a(k)
+            if j <= NQ:
                 g, c = divmod(k + 1, 2)
                 if g < G:
                     quantise_msg(g, c)
                 g, c = divmod(k + 2, 2)
-                if g < G:
+                if 2 <= g < G:
                     regroup_msg(g, c)
+            relu(j - 2, "gpsimd")
+            relu(j - 2, "vector")
+            for kk in range(stores_by(j - 1), stores_by(j)):
+                store(kk)
+            if j <= NQ:
                 self_term(k, woven)
+                if j == NQ - 1:
+                    quantise_a(j)
+            relu(j - 2, "scalar")
+            if j <= NQ:
                 aggregate(k)

@@ -21,17 +21,21 @@ AHEAD = 3
 ST_LAG = 4
 PERM = 2
 FIRST_PERM = 4
+V_GRAPHS = 3
+SCALAR_SELF = (0, 15)
 VECTOR_TILES = [(0, 1), (0, 3)]
 
 
 def relu_engine(k, pair):
+    if k == 0:
+        return "scalar"
     if k >= 14:
         return ("gpsimd", "vector", "scalar", "vector")[2 * (k - 14) + pair]
     return ("vector", "gpsimd")[pair]
 
 
 def perms(j):
-    return 0 if j < FIRST_PERM else PERM
+    return 0 if j < FIRST_PERM else PERM - (j + 1) % 2
 
 
 def tile_gcnstacking_pb_t_kernel(tc, A, msg, h, Ws, b, out):
@@ -78,10 +82,13 @@ def tile_gcnstacking_pb_t_kernel(tc, A, msg, h, Ws, b, out):
                 load_a(1, 4)
                 load_msg(0)
             else:
-                load_msg(g)
-                load_a(2 * g, 1)
+                if g > 1:
+                    load_msg(g)
+                load_a(2 * g, 4 if g == 1 else 1)
                 load_h(g)
-                load_a(2 * g + 1, 1)
+                if g == 1:
+                    load_msg(g)
+                load_a(2 * g + 1, 4 if g == 1 else 1)
 
         def a_tile_steps(j, t):
             grp_words = a_grp[j][:].bitcast(F32)
@@ -147,7 +154,7 @@ def tile_gcnstacking_pb_t_kernel(tc, A, msg, h, Ws, b, out):
 
         def regroup_msg(g, c):
             m_grp[g, c] = work.tile([P, 1024], BF16, name="m_grp%d" % c, tag="m_grp%d" % c, bufs=1, align_bytes=64)
-            if g == 0:
+            if g < V_GRAPHS:
                 nc.vector.tensor_copy(
                     out=m_grp[g, c][:].rearrange("p (n i t) -> p n t i", n=64, i=4, t=4),
                     in_=m_raw[g][:, 1024 * c:1024 * (c + 1)].rearrange("p (t n i) -> p n t i", t=4, n=64, i=4),
@@ -173,7 +180,7 @@ def tile_gcnstacking_pb_t_kernel(tc, A, msg, h, Ws, b, out):
                     bank = psum.tile([P, 512], F32, name="acc", tag="acc", bufs=3)
                 for tt in range(2):
                     t = 2 * pair + tt
-                    if k == NQ - 1:
+                    if k in SCALAR_SELF:
                         nc.tensor.matmul(out=bank[:, 256 * tt:256 * (tt + 1)], lhsT=ones[:], rhs=b_row[:], start=True, stop=False)
                     for e in range(2):
                         if n < len(woven):
@@ -183,11 +190,11 @@ def tile_gcnstacking_pb_t_kernel(tc, A, msg, h, Ws, b, out):
                             out=bank[:, 256 * tt:256 * (tt + 1)],
                             lhsT=hT_bf[:, 256 * t + e:256 * (t + 1):2],
                             rhs=wsT[:, 256 * e:256 * (e + 1)],
-                            start=(e == 0 and k < NQ - 1),
+                            start=(e == 0 and k not in SCALAR_SELF),
                             stop=(e == 1),
                         )
                 half = y[k][:, 512 * pair:512 * (pair + 1)]
-                if k == NQ - 1:
+                if k in SCALAR_SELF:
                     nc.scalar.copy(out=half, in_=bank[:])
                 else:
                     nc.vector.tensor_tensor(out=half, in0=bank[:], in1=bias2[:], op=ADD)
@@ -256,7 +263,7 @@ def tile_gcnstacking_pb_t_kernel(tc, A, msg, h, Ws, b, out):
             )
 
         def make_bias():
-            b_bank = psum.tile([P, 512], F32, name="acc", tag="acc", bufs=3)
+            b_bank = psum.tile([P, 512], F32, name="ht", tag="ht", bufs=1)
             nc.tensor.matmul(out=b_bank[:, 0:256], lhsT=ones[:], rhs=b_row[:], start=True, stop=True)
             for r in range(2):
                 nc.vector.tensor_copy(out=bias2[:, 256 * r:256 * (r + 1)], in_=b_bank[:, 0:256])
@@ -268,7 +275,8 @@ def tile_gcnstacking_pb_t_kernel(tc, A, msg, h, Ws, b, out):
         new_group(0)
         for t in range(4):
             run(a_tile_steps(0, t))
-        make_weights()
+            if t == 0:
+                make_weights()
         quantise_a(0)
         for j in range(2):
             run(h_steps(j))
@@ -280,10 +288,11 @@ def tile_gcnstacking_pb_t_kernel(tc, A, msg, h, Ws, b, out):
         for c in range(2):
             quantise_msg(0, c)
         make_bias()
+        self_term(0, [])
+        quantise_a(1)
+        aggregate(0)
         for c in range(2):
             regroup_msg(1, c)
-        self_term(0, [])
-        aggregate(0)
 
         for j in range(2, NQ + 2):
             k = j - 1
@@ -303,7 +312,7 @@ def tile_gcnstacking_pb_t_kernel(tc, A, msg, h, Ws, b, out):
                         permute(j + 1, tt)
                 for t in range(2, 4):
                     woven += a_tile_steps(j, t)
-            if j < NQ:
+            if 2 < j < NQ:
                 quantise_a(k)
             if j <= NQ:
                 g, c = divmod(k + 1, 2)

@@ -27,11 +27,11 @@ VECTOR_TILES = [(0, 1), (0, 3)]
 
 
 def relu_engine(k, pair):
-    if k == 0:
-        return "scalar"
-    if k >= 14:
-        return ("gpsimd", "vector", "scalar", "vector")[2 * (k - 14) + pair]
-    return ("vector", "gpsimd")[pair]
+    if k == 0 or k >= 14:
+        return "gpsimd" if (k, pair) == (14, 0) else "scalar"
+    if pair == 1:
+        return "gpsimd"
+    return "scalar" if k % 2 else "vector"
 
 
 def perms(j):
@@ -307,6 +307,7 @@ def tile_gcnstacking_pb_t_kernel(tc, A, msg, h, Ws, b, out):
                     run(a_tile_steps(j, t))
                 if j == 2:
                     run(h_steps(j))
+                relu(j - 2, "scalar")
                 if FIRST_PERM <= j + 1 < NQ:
                     for tt in range(4 - perms(j + 1), 4):
                         permute(j + 1, tt)
@@ -329,6 +330,7 @@ def tile_gcnstacking_pb_t_kernel(tc, A, msg, h, Ws, b, out):
                 self_term(k, woven)
                 if j == NQ - 1:
                     quantise_a(j)
-            relu(j - 2, "scalar")
+            if j >= NQ:
+                relu(j - 2, "scalar")
             if j <= NQ:
                 aggregate(k)

from contextlib import ExitStack

import concourse.mybir as mybir
from concourse.masks import make_identity

FLOPS = 2 * 8 * 1024 * 256 * (1024 + 256)

F32 = mybir.dt.float32
BF16 = mybir.dt.bfloat16
U32 = mybir.dt.uint32
U8 = mybir.dt.uint8
FP8X4 = mybir.dt.float8_e4m3fn_x4
ADD = mybir.AluOpType.add
MULT = mybir.AluOpType.mult
RELU = mybir.ActivationFunctionType.Relu
MIN = mybir.AluOpType.min
MAX = mybir.AluOpType.max
F32_MAX = (2.0 - 2.0**-23) * 2.0**127
P = 128
AHEAD = 3
ST_LAG = 4
PERM = 2
FIRST_PERM = 4
V_GRAPHS = 3
SCALAR_SELF = (0, 15)
VECTOR_TILES = [(0, 1), (0, 3)]


def relu_engine(k, pair):
    if k == 0 or k >= 14:
        return "gpsimd" if (k, pair) == (14, 0) else "scalar"
    if pair == 1:
        return "gpsimd"
    return "scalar" if k % 2 else "vector"


def perms(j):
    return 0 if j < FIRST_PERM else PERM - (j + 1) % 2


def tile_gcnstacking_pb_t_kernel(tc, A, msg, h, Ws, b, out):
    nc = tc.nc
    G = 8
    NQ = 2 * G

    a_view = A.rearrange("g (p q t) k -> g q p (t k)", p=P, q=2, t=4)
    o_view = out.rearrange("g (p q t) c -> g q p (t c)", p=P, q=2, t=4)
    h_view = h.rearrange("g (p r) c -> g p (r c)", p=P)
    m_view = msg.rearrange("g (c p t) n -> g p c (t n)", c=2, p=P, t=4)

    with ExitStack() as ctx:
        const = ctx.enter_context(tc.tile_pool(name="const", bufs=1))
        raw = ctx.enter_context(tc.tile_pool(name="raw", bufs=4))
        work = ctx.enter_context(tc.tile_pool(name="work", bufs=3))
        psum = ctx.enter_context(tc.psum_pool(name="psum", bufs=1))
        ctx.enter_context(tc.manual_schedule())

        a_raw, h_raw, m_raw = {}, {}, {}
        a_per = {}
        a_grp, a_cod, a_scl = {}, {}, {}
        m_grp, m_cod, m_scl = {}, {}, {}
        hT, y = {}, {}

        def load_msg(g):
            m_raw[g] = raw.tile([P, 2048], BF16, name="m_raw", tag="m_raw", bufs=AHEAD + 2)
            nc.sync.dma_start(out=m_raw[g][:].rearrange("p (c x) -> p c x", c=2), in_=m_view[g])

        def load_h(g):
            h_raw[g] = raw.tile([P, 2048], BF16, name="h_raw", tag="h_raw", bufs=AHEAD + 1)
            nc.sync.dma_start(out=h_raw[g][:], in_=h_view[g])

        def load_a(j, pieces):
            a_raw[j] = raw.tile([P, 4096], BF16, name="a_raw", tag="a_raw", bufs=2 * (AHEAD + 1))
            w = 4096 // pieces
            for i in range(pieces):
                nc.sync.dma_start(out=a_raw[j][:, w * i:w * (i + 1)], in_=a_view[j // 2, j % 2][:, w * i:w * (i + 1)])

        def load_graph(g):
            if g == 0:
                load_a(0, 4)
                load_h(0)
                load_a(1, 4)
                load_msg(0)
            else:
                if g > 1:
                    load_msg(g)
                load_a(2 * g, 4 if g == 1 else 1)
                load_h(g)
                if g == 1:
                    load_msg(g)
                load_a(2 * g + 1, 4 if g == 1 else 1)

        def a_tile_steps(j, t):
            grp_words = a_grp[j][:].bitcast(F32)
            bank = psum.tile([P, 512], F32, name="at", tag="at", bufs=4)

            def one(s):
                c, u = divmod(s, 2)
                if (j, t) in a_per:
                    lo = 256 * u + 128 * c
                    words = a_per[j, t][:, lo:lo + 128]
                else:
                    lo = 512 * t + 256 * c
                    words = a_raw[j][:].bitcast(F32)[:, lo + u:lo + 256:2]
                nc.tensor.transpose(out=bank[:, 128 * s:128 * (s + 1)], in_=words, identity=ident[:])
                if s == 3:
                    copy = nc.vector.tensor_copy if (j, t) in VECTOR_TILES else nc.scalar.copy
                    copy(
                        out=grp_words[:, 512 * t:512 * (t + 1)].rearrange("p (c i u) -> p c i u", c=2, i=128, u=2),
                        in_=bank[:].rearrange("p (c u i) -> p c i u", c=2, u=2, i=128),
                    )

            return [(one, s) for s in range(4)]

        def permute(j, t):
            a_per[j, t] = work.tile([P, 512], F32, name="a_per", tag="a_per", bufs=2 * PERM)
            nc.scalar.copy(
                out=a_per[j, t][:].rearrange("p (u w) -> p u w", u=2),
                in_=a_raw[j][:].bitcast(F32)[:, 512 * t:512 * (t + 1)].rearrange("p (w u) -> p u w", u=2),
            )

        def h_steps(j):
            g, q = divmod(j, 2)
            h_words = h_raw[g][:].bitcast(F32)
            if j == 1:
                bank = psum.tile([P, 512], F32, name="acc", tag="acc", bufs=3)
            else:
                bank = psum.tile([P, 512], F32, name="ht", tag="ht", bufs=1)
            hT[j] = work.tile([P, 512], F32, name="hT", tag="hT")

            def one(t):
                lo = 128 * (4 * q + t)
                nc.tensor.transpose(out=bank[:, 128 * t:128 * (t + 1)], in_=h_words[:, lo:lo + 128], identity=ident[:])
                if t == 3:
                    nc.scalar.copy(out=hT[j][:], in_=bank[:])

            return [(one, t) for t in range(4)]

        def run(steps):
            for fn, arg in steps:
                fn(arg)

        def new_group(j):
            a_grp[j] = work.tile([P, 4096], BF16, name="a_grp", tag="a_grp", align_bytes=64)

        def quantise_a(k):
            a_cod[k] = work.tile([P, 1024], U32, name="a_cod", tag="a_cod", align_bytes=64)
            a_scl[k] = work.tile([P, 1024], U8, name="a_scl", tag="a_scl", align_bytes=64)
            for lo in range(0, 1024, 512 if k == NQ - 1 else 1024):
                cols = slice(lo, lo + (512 if k == NQ - 1 else 1024))
                nc.vector.quantize_mx(
                    out=a_cod[k][:, cols].bitcast(FP8X4), scales=a_scl[k][:, cols], in_=a_grp[k][:, 4 * cols.start:4 * cols.stop]
                )

        def regroup_msg(g, c):
            m_grp[g, c] = work.tile([P, 1024], BF16, name="m_grp%d" % c, tag="m_grp%d" % c, bufs=1, align_bytes=64)
            if g < V_GRAPHS:
                nc.vector.tensor_copy(
                    out=m_grp[g, c][:].rearrange("p (n i t) -> p n t i", n=64, i=4, t=4),
                    in_=m_raw[g][:, 1024 * c:1024 * (c + 1)].rearrange("p (t n i) -> p n t i", t=4, n=64, i=4),
                )
            else:
                src = m_raw[g][:, 1024 * c:1024 * (c + 1)].rearrange("p (t n) -> p n t", t=4)
                dst = m_grp[g, c][:].rearrange("p (n t) -> p n t", t=4)
                nc.gpsimd.tensor_scalar(out=dst, in0=src, scalar1=1.0, scalar2=0.0, op0=MULT, op1=ADD)

        def quantise_msg(g, c):
            m_cod[g, c] = work.tile([P, 256], U32, name="m_cod%d" % c, tag="m_cod%d" % c, align_bytes=64)
            m_scl[g, c] = work.tile([P, 256], U8, name="m_scl%d" % c, tag="m_scl%d" % c, align_bytes=64)
            nc.vector.quantize_mx(out=m_cod[g, c][:].bitcast(FP8X4), scales=m_scl[g, c][:], in_=m_grp[g, c][:])

        def self_term(k, woven):
            y[k] = work.tile([P, 1024], F32, name="y", tag="y", bufs=12)
            hT_bf = hT[k][:].bitcast(BF16)
            n = 0
            for pair in range(2):
                if k == NQ - 1:
                    bank = psum.tile([P, 512], F32, name="at", tag="at", bufs=4)
                else:
                    bank = psum.tile([P, 512], F32, name="acc", tag="acc", bufs=3)
                for tt in range(2):
                    t = 2 * pair + tt
                    if k in SCALAR_SELF:
                        nc.tensor.matmul(out=bank[:, 256 * tt:256 * (tt + 1)], lhsT=ones[:], rhs=b_row[:], start=True, stop=False)
                    for e in range(2):
                        if n < len(woven):
                            run(woven[n:n + 1])
                        n += 1
                        nc.tensor.matmul(
                            out=bank[:, 256 * tt:256 * (tt + 1)],
                            lhsT=hT_bf[:, 256 * t + e:256 * (t + 1):2],
                            rhs=wsT[:, 256 * e:256 * (e + 1)],
                            start=(e == 0 and k not in SCALAR_SELF),
                            stop=(e == 1),
                        )
                half = y[k][:, 512 * pair:512 * (pair + 1)]
                if k in SCALAR_SELF:
                    nc.scalar.copy(out=half, in_=bank[:])
                else:
                    nc.vector.tensor_tensor(out=half, in0=bank[:], in1=bias2[:], op=ADD)

        def aggregate(k):
            g = k // 2
            for pair in range(2):
                bank = psum.tile([P, 512], F32, name="acc", tag="acc", bufs=3)
                for tt in range(2):
                    t = 2 * pair + tt
                    for c in range(2):
                        lo = 256 * t + 128 * c
                        nc.tensor.matmul_mx(
                            out=bank[:, 256 * tt:256 * (tt + 1)],
                            lhsT=a_cod[k][:, lo:lo + 128].bitcast(FP8X4),
                            lhsT_scale=a_scl[k][:, lo:lo + 128],
                            rhs=m_cod[g, c][:].bitcast(FP8X4),
                            rhs_scale=m_scl[g, c][:],
                            start=(c == 0),
                            stop=(c == 1),
                        )
                half = y[k][:, 512 * pair:512 * (pair + 1)]
                nc.vector.tensor_tensor(out=half, in0=bank[:], in1=half, op=ADD)

        def relu(k, engine):
            for pair in range(2):
                if relu_engine(k, pair) != engine:
                    continue
                half = y[k][:, 512 * pair:512 * (pair + 1)]
                if engine == "scalar":
                    nc.scalar.activation(out=half, in_=half, func=RELU)
                elif engine == "vector":
                    nc.vector.tensor_scalar(out=half, in0=half, scalar1=0.0, scalar2=None, op0=MAX)
                else:
                    nc.gpsimd.tensor_scalar(out=half, in0=half, scalar1=F32_MAX, scalar2=0.0, op0=MIN, op1=MAX)
                if k >= NQ - 2:
                    nc.sync.dma_start(out=o_view[k // 2, k % 2][:, 512 * pair:512 * (pair + 1)], in_=half)

        def store(k):
            nc.sync.dma_start(out=o_view[k // 2, k % 2], in_=y[k][:])

        ident = const.tile([P, P], F32, name="ident")
        make_identity(nc, ident[:])
        w_raw = const.tile([P, 512], BF16, name="w_raw")
        nc.scalar.dma_start(out=w_raw[:].rearrange("p (o c) -> p o c", o=2), in_=Ws.rearrange("(o p) c -> p o c", p=P))
        b_row = const.tile([P, 256], BF16, name="b_row")
        nc.vector.memset(b_row[:], 0.0)
        nc.scalar.dma_start(out=b_row[0:1, :], in_=b.unsqueeze(0))
        ones = const.tile([P, P], BF16, name="ones")
        nc.vector.memset(ones[:], 1.0)

        for g in range(AHEAD + 1):
            load_graph(g)

        wsT = const.tile([P, 512], BF16, name="wsT")
        bias2 = const.tile([P, 512], F32, name="bias2")

        def make_weights():
            w_words = w_raw[:].bitcast(F32)
            w_bank = psum.tile([P, 512], F32, name="ht", tag="ht", bufs=1)
            for o in range(2):
                nc.tensor.transpose(out=w_bank[:, 128 * o:128 * (o + 1)], in_=w_words[:, 128 * o:128 * (o + 1)], identity=ident[:])
            nc.vector.tensor_copy(
                out=wsT[:].rearrange("p (e o) -> p e o", e=2),
                in_=w_bank[:, 0:256].bitcast(BF16).rearrange("p (o e) -> p e o", e=2),
            )

        def make_bias():
            b_bank = psum.tile([P, 512], F32, name="ht", tag="ht", bufs=1)
            nc.tensor.matmul(out=b_bank[:, 0:256], lhsT=ones[:], rhs=b_row[:], start=True, stop=True)
            for r in range(2):
                nc.vector.tensor_copy(out=bias2[:, 256 * r:256 * (r + 1)], in_=b_bank[:, 0:256])

        def stores_by(j):
            lag = ST_LAG if j <= 2 * (G - 1 - AHEAD) else 2
            return max(0, min(j - lag + 1, NQ - 2))

        new_group(0)
        for t in range(4):
            run(a_tile_steps(0, t))
            if t == 0:
                make_weights()
        quantise_a(0)
        for j in range(2):
            run(h_steps(j))
        new_group(1)
        for t in range(4):
            run(a_tile_steps(1, t))
        for c in range(2):
            regroup_msg(0, c)
        for c in range(2):
            quantise_msg(0, c)
        make_bias()
        self_term(0, [])
        quantise_a(1)
        aggregate(0)
        for c in range(2):
            regroup_msg(1, c)

        for j in range(2, NQ + 2):
            k = j - 1
            if j % 2 == 0 and j // 2 + AHEAD < G:
                load_graph(j // 2 + AHEAD)
            woven = []
            if j < NQ:
                new_group(j)
                if j > 2:
                    run(h_steps(j))
                for t in range(2):
                    run(a_tile_steps(j, t))
                if j == 2:
                    run(h_steps(j))
                relu(j - 2, "scalar")
                if FIRST_PERM <= j + 1 < NQ:
                    for tt in range(4 - perms(j + 1), 4):
                        permute(j + 1, tt)
                for t in range(2, 4):
                    woven += a_tile_steps(j, t)
            if 2 < j < NQ:
                quantise_a(k)
            if j <= NQ:
                g, c = divmod(k + 1, 2)
                if g < G:
                    quantise_msg(g, c)
                g, c = divmod(k + 2, 2)
                if 2 <= g < G:
                    regroup_msg(g, c)
            relu(j - 2, "gpsimd")
            relu(j - 2, "vector")
            for kk in range(stores_by(j - 1), stores_by(j)):
                store(kk)
            if j <= NQ:
                self_term(k, woven)
                if j == NQ - 1:
                    quantise_a(j)
            if j >= NQ:
                relu(j - 2, "scalar")
            if j <= NQ:
                aggregate(k)
